import numpy as np
import ml_dtypes

BF16 = ml_dtypes.bfloat16


def bf(x):
    return np.asarray(x, np.float32).astype(BF16)


def f32(x):
    return np.asarray(x, np.float32)


def f64(x):
    return np.asarray(x).astype(np.float64)


def striped(idx):
    return np.tile(idx.reshape(-1, 16).T, (8, 1))


C, S, N, E = 128, 1024, 128, 64


def setup_inputs():
    amp = np.sqrt(6.0 / C)
    x = f32(amp * np.random.uniform(size=(C, S)) * (0.5 + np.random.uniform(size=(1, S))))
    other = f32(amp * np.random.uniform(size=(C, N)) * (0.5 + np.random.uniform(size=(1, N))))
    return {"x": x, "other": other, "offs": striped(np.random.permutation(np.tile(np.arange(S), 2))[:N])}


def reference(x, other, offs):
    idx = offs[:16].T.reshape(-1)
    d = (f64(x)[:, idx] * f64(other)).sum(axis=0, keepdims=True)
    return np.concatenate([np.log(1.0 - np.exp(-d[:, :E])), -d[:, E:]], axis=1)

@@ -1,0 +1,45 @@
+import concourse.mybir as mybir
+
+F32 = mybir.dt.float32
+U16 = mybir.dt.uint16
+ACT = mybir.ActivationFunctionType
+
+C = 128
+S = 1024
+N = 128
+E = 64
+
+FLOPS = 2 * C * N
+
+
+def tile_graphloglikelihood_kernel(tc, x, other, offs, out):
+    nc = tc.nc
+    with (
+        tc.tile_pool(name="held", bufs=1) as held,
+        tc.psum_pool(name="psum", bufs=1) as psum,
+    ):
+        offsets = held.tile([C, N // 16], U16, name="offsets")
+        nc.sync.dma_start(offsets[:], offs)
+        nodes = held.tile([C, S], F32, name="nodes")
+        nc.sync.dma_start(nodes[:], x)
+        partners = held.tile([C, N], F32, name="partners")
+        nc.scalar.dma_start(partners[:], other)
+
+        ones = held.tile([C, 1], F32, name="ones")
+        nc.vector.memset(ones[:], 1.0)
+
+        products = held.tile([C, N], F32, name="products")
+        nc.vector.tensor_tensor(
+            products[:], nodes[:].indirect(offsets[:]), partners[:], mybir.AluOpType.mult
+        )
+
+        d = psum.tile([1, N], F32, name="d")
+        nc.tensor.matmul(d[:], ones[:], products[:], start=True, stop=True)
+
+        terms = held.tile([1, N], F32, name="terms")
+        miss = held.tile([1, E], F32, name="miss")
+        nc.scalar.activation(miss[:], d[:, 0:E], ACT.Exp, scale=-1.0)
+        nc.scalar.activation(terms[:, 0:E], miss[:], ACT.Ln, bias=1.0, scale=-1.0)
+        nc.scalar.mul(terms[:, E:N], d[:, E:N], -1.0)
+
+        nc.sync.dma_start(out, terms[:])

@@ -28,18 +28,22 @@ def tile_graphloglikelihood_kernel(tc, x, other, offs, out):
         ones = held.tile([C, 1], F32, name="ones")
         nc.vector.memset(ones[:], 1.0)
 
-        products = held.tile([C, N], F32, name="products")
-        nc.vector.tensor_tensor(
-            products[:], nodes[:].indirect(offsets[:]), partners[:], mybir.AluOpType.mult
-        )
-
-        d = psum.tile([1, N], F32, name="d")
-        nc.tensor.matmul(d[:], ones[:], products[:], start=True, stop=True)
+        sums = {}
+        for kind, lo, hi in (("edges", 0, E), ("others", E, N)):
+            products = held.tile([C, hi - lo], F32, name=f"products_{kind}")
+            nc.vector.tensor_tensor(
+                products[:],
+                nodes[:].indirect(offsets[:, lo // 16 : hi // 16]),
+                partners[:, lo:hi],
+                mybir.AluOpType.mult,
+            )
+            sums[kind] = psum.tile([1, hi - lo], F32, name=f"d_{kind}")
+            nc.tensor.matmul(sums[kind][:], ones[:], products[:], start=True, stop=True)
 
         terms = held.tile([1, N], F32, name="terms")
         miss = held.tile([1, E], F32, name="miss")
-        nc.scalar.activation(miss[:], d[:, 0:E], ACT.Exp, scale=-1.0)
+        nc.scalar.activation(miss[:], sums["edges"][:], ACT.Exp, scale=-1.0)
         nc.scalar.activation(terms[:, 0:E], miss[:], ACT.Ln, bias=1.0, scale=-1.0)
-        nc.scalar.mul(terms[:, E:N], d[:, E:N], -1.0)
+        nc.vector.tensor_scalar_mul(terms[:, E:N], sums["others"][:], -1.0)
 
         nc.sync.dma_start(out, terms[:])

@@ -18,12 +18,12 @@ def tile_graphloglikelihood_kernel(tc, x, other, offs, out):
         tc.tile_pool(name="held", bufs=1) as held,
         tc.psum_pool(name="psum", bufs=1) as psum,
     ):
+        nodes = held.tile([C, S], F32, name="nodes")
+        nc.scalar.dma_start(nodes[:], x)
         offsets = held.tile([C, N // 16], U16, name="offsets")
         nc.sync.dma_start(offsets[:], offs)
-        nodes = held.tile([C, S], F32, name="nodes")
-        nc.sync.dma_start(nodes[:], x)
         partners = held.tile([C, N], F32, name="partners")
-        nc.scalar.dma_start(partners[:], other)
+        nc.sync.dma_start(partners[:], other)
 
         ones = held.tile([C, 1], F32, name="ones")
         nc.vector.memset(ones[:], 1.0)

@@ -1,8 +1,11 @@
+import math
+
 import concourse.mybir as mybir
 
 F32 = mybir.dt.float32
 U16 = mybir.dt.uint16
 ACT = mybir.ActivationFunctionType
+ALU = mybir.AluOpType
 
 C = 128
 S = 1024
@@ -27,6 +30,8 @@ def tile_graphloglikelihood_kernel(tc, x, other, offs, out):
 
         ones = held.tile([C, 1], F32, name="ones")
         nc.vector.memset(ones[:], 1.0)
+        inverse_e = held.tile([1, E], F32, name="inverse_e")
+        nc.gpsimd.memset(inverse_e[:], 1.0 / math.e)
 
         sums = {}
         for kind, lo, hi in (("edges", 0, E), ("others", E, N)):
@@ -35,14 +40,16 @@ def tile_graphloglikelihood_kernel(tc, x, other, offs, out):
                 products[:],
                 nodes[:].indirect(offsets[:, lo // 16 : hi // 16]),
                 partners[:, lo:hi],
-                mybir.AluOpType.mult,
+                ALU.mult,
             )
             sums[kind] = psum.tile([1, hi - lo], F32, name=f"d_{kind}")
             nc.tensor.matmul(sums[kind][:], ones[:], products[:], start=True, stop=True)
 
         terms = held.tile([1, N], F32, name="terms")
+        d_edges = held.tile([1, E], F32, name="d_edges")
+        nc.vector.tensor_copy(d_edges[:], sums["edges"][:])
         miss = held.tile([1, E], F32, name="miss")
-        nc.scalar.activation(miss[:], sums["edges"][:], ACT.Exp, scale=-1.0)
+        nc.gpsimd.tensor_tensor(miss[:], inverse_e[:], d_edges[:], ALU.pow)
         nc.scalar.activation(terms[:, 0:E], miss[:], ACT.Ln, bias=1.0, scale=-1.0)
         nc.vector.tensor_scalar_mul(terms[:, E:N], sums["others"][:], -1.0)
 

@@ -1,6 +1,7 @@
 import math
 
 import concourse.mybir as mybir
+from concourse.masks import make_identity
 
 F32 = mybir.dt.float32
 U16 = mybir.dt.uint16
@@ -11,6 +12,8 @@ C = 128
 S = 1024
 N = 128
 E = 64
+P = 128
+Q = 32
 
 FLOPS = 2 * C * N
 
@@ -30,27 +33,43 @@ def tile_graphloglikelihood_kernel(tc, x, other, offs, out):
 
         ones = held.tile([C, 1], F32, name="ones")
         nc.vector.memset(ones[:], 1.0)
-        inverse_e = held.tile([1, E], F32, name="inverse_e")
+        inverse_e = held.tile([E, 1], F32, name="inverse_e")
         nc.gpsimd.memset(inverse_e[:], 1.0 / math.e)
+        identity = held.tile([P, P], F32, name="identity")
+        make_identity(nc, identity[:])
 
-        sums = {}
-        for kind, lo, hi in (("edges", 0, E), ("others", E, N)):
-            products = held.tile([C, hi - lo], F32, name=f"products_{kind}")
-            nc.vector.tensor_tensor(
-                products[:],
-                nodes[:].indirect(offsets[:, lo // 16 : hi // 16]),
-                partners[:, lo:hi],
-                ALU.mult,
+        products_edges = held.tile([C, E], F32, name="products_edges")
+        nc.vector.tensor_tensor(
+            products_edges[:],
+            nodes[:].indirect(offsets[:, 0 : E // 16]),
+            partners[:, 0:E],
+            ALU.mult,
+        )
+        products_others = held.tile([C, N - E], F32, name="products_others")
+        nc.vector.tensor_tensor(
+            products_others[:],
+            nodes[:].indirect(offsets[:, E // 16 : N // 16]),
+            partners[:, E:N],
+            ALU.mult,
+        )
+
+        d_edges = psum.tile([E, 1], F32, name="d_edges")
+        for q in range(0, E, Q):
+            nc.tensor.matmul(
+                d_edges[q : q + Q, :], products_edges[:, q : q + Q], ones[:], start=True, stop=True
             )
-            sums[kind] = psum.tile([1, hi - lo], F32, name=f"d_{kind}")
-            nc.tensor.matmul(sums[kind][:], ones[:], products[:], start=True, stop=True)
-
+        d_edges_sbuf = held.tile([E, 1], F32, name="d_edges_sbuf")
+        nc.vector.tensor_copy(d_edges_sbuf[:], d_edges[:])
+        miss = held.tile([P, 1], F32, name="miss")
+        nc.gpsimd.memset(miss[:], 0.0)
+        nc.gpsimd.tensor_tensor(miss[0:E, :], inverse_e[:], d_edges_sbuf[:], ALU.pow)
+        miss_row = psum.tile([1, P], F32, name="miss_row")
+        nc.tensor.transpose(miss_row[:], miss[:], identity[:])
         terms = held.tile([1, N], F32, name="terms")
-        d_edges = held.tile([1, E], F32, name="d_edges")
-        nc.vector.tensor_copy(d_edges[:], sums["edges"][:])
-        miss = held.tile([1, E], F32, name="miss")
-        nc.gpsimd.tensor_tensor(miss[:], inverse_e[:], d_edges[:], ALU.pow)
-        nc.scalar.activation(terms[:, 0:E], miss[:], ACT.Ln, bias=1.0, scale=-1.0)
-        nc.vector.tensor_scalar_mul(terms[:, E:N], sums["others"][:], -1.0)
+        nc.scalar.activation(terms[:, 0:E], miss_row[:, 0:E], ACT.Ln, bias=1.0, scale=-1.0)
+
+        d_others = psum.tile([1, N - E], F32, name="d_others")
+        nc.tensor.matmul(d_others[:], ones[:], products_others[:], start=True, stop=True)
+        nc.vector.tensor_scalar_mul(terms[:, E:N], d_others[:], -1.0)
 
         nc.sync.dma_start(out, terms[:])

@@ -14,6 +14,7 @@ N = 128
 E = 64
 P = 128
 Q = 32
+PITCH = 96
 
 FLOPS = 2 * C * N
 
@@ -65,11 +66,14 @@ def tile_graphloglikelihood_kernel(tc, x, other, offs, out):
         nc.gpsimd.tensor_tensor(miss[0:E, :], inverse_e[:], d_edges_sbuf[:], ALU.pow)
         miss_row = psum.tile([1, P], F32, name="miss_row")
         nc.tensor.transpose(miss_row[:], miss[:], identity[:])
-        terms = held.tile([1, N], F32, name="terms")
+        terms = held.tile([1, 2 * PITCH], F32, name="terms")
         nc.scalar.activation(terms[:, 0:E], miss_row[:, 0:E], ACT.Ln, bias=1.0, scale=-1.0)
 
         d_others = psum.tile([1, N - E], F32, name="d_others")
         nc.tensor.matmul(d_others[:], ones[:], products_others[:], start=True, stop=True)
-        nc.vector.tensor_scalar_mul(terms[:, E:N], d_others[:], -1.0)
+        nc.vector.tensor_scalar_mul(terms[:, PITCH : PITCH + E], d_others[:], -1.0)
 
-        nc.sync.dma_start(out, terms[:])
+        nc.sync.dma_start(
+            out.rearrange("o (h j) -> o h j", h=2),
+            terms[:].rearrange("o (h w) -> o h w", h=2)[:, :, 0:E],
+        )

@@ -34,6 +34,8 @@ def tile_graphloglikelihood_kernel(tc, x, other, offs, out):
 
         ones = held.tile([C, 1], F32, name="ones")
         nc.vector.memset(ones[:], 1.0)
+        warm = held.tile([C, 1], F32, name="warm")
+        nc.scalar.activation(warm[:], ones[:], ACT.Ln)
         inverse_e = held.tile([E, 1], F32, name="inverse_e")
         nc.gpsimd.memset(inverse_e[:], 1.0 / math.e)
         identity = held.tile([P, P], F32, name="identity")
@@ -60,7 +62,7 @@ def tile_graphloglikelihood_kernel(tc, x, other, offs, out):
                 d_edges[q : q + Q, :], products_edges[:, q : q + Q], ones[:], start=True, stop=True
             )
         d_edges_sbuf = held.tile([E, 1], F32, name="d_edges_sbuf")
-        nc.vector.tensor_copy(d_edges_sbuf[:], d_edges[:])
+        nc.scalar.copy(d_edges_sbuf[:], d_edges[:])
         miss = held.tile([P, 1], F32, name="miss")
         nc.gpsimd.memset(miss[:], 0.0)
         nc.gpsimd.tensor_tensor(miss[0:E, :], inverse_e[:], d_edges_sbuf[:], ALU.pow)

@@ -37,7 +37,9 @@ def tile_graphloglikelihood_kernel(tc, x, other, offs, out):
         warm = held.tile([C, 1], F32, name="warm")
         nc.scalar.activation(warm[:], ones[:], ACT.Ln)
         inverse_e = held.tile([E, 1], F32, name="inverse_e")
-        nc.gpsimd.memset(inverse_e[:], 1.0 / math.e)
+        nc.vector.memset(inverse_e[:], 1.0 / math.e)
+        miss = held.tile([P, 1], F32, name="miss")
+        nc.vector.memset(miss[:], 0.0)
         identity = held.tile([P, P], F32, name="identity")
         make_identity(nc, identity[:])
 
@@ -63,8 +65,6 @@ def tile_graphloglikelihood_kernel(tc, x, other, offs, out):
             )
         d_edges_sbuf = held.tile([E, 1], F32, name="d_edges_sbuf")
         nc.scalar.copy(d_edges_sbuf[:], d_edges[:])
-        miss = held.tile([P, 1], F32, name="miss")
-        nc.gpsimd.memset(miss[:], 0.0)
         nc.gpsimd.tensor_tensor(miss[0:E, :], inverse_e[:], d_edges_sbuf[:], ALU.pow)
         miss_row = psum.tile([1, P], F32, name="miss_row")
         nc.tensor.transpose(miss_row[:], miss[:], identity[:])

@@ -27,10 +27,10 @@ def tile_graphloglikelihood_kernel(tc, x, other, offs, out):
     ):
         nodes = held.tile([C, S], F32, name="nodes")
         nc.scalar.dma_start(nodes[:], x)
-        offsets = held.tile([C, N // 16], U16, name="offsets")
-        nc.sync.dma_start(offsets[:], offs)
         partners = held.tile([C, N], F32, name="partners")
         nc.sync.dma_start(partners[:], other)
+        offsets = held.tile([C, N // 16], U16, name="offsets")
+        nc.sync.dma_start(offsets[:], offs)
 
         ones = held.tile([C, 1], F32, name="ones")
         nc.vector.memset(ones[:], 1.0)
@@ -43,6 +43,9 @@ def tile_graphloglikelihood_kernel(tc, x, other, offs, out):
         identity = held.tile([P, P], F32, name="identity")
         make_identity(nc, identity[:])
 
+        partners_negated = held.tile([C, N - E], F32, name="partners_negated")
+        nc.vector.tensor_scalar_mul(partners_negated[:], partners[:, E:N], -1.0)
+
         products_edges = held.tile([C, E], F32, name="products_edges")
         nc.vector.tensor_tensor(
             products_edges[:],
@@ -54,7 +57,7 @@ def tile_graphloglikelihood_kernel(tc, x, other, offs, out):
         nc.vector.tensor_tensor(
             products_others[:],
             nodes[:].indirect(offsets[:, E // 16 : N // 16]),
-            partners[:, E:N],
+            partners_negated[:],
             ALU.mult,
         )
 
@@ -71,9 +74,9 @@ def tile_graphloglikelihood_kernel(tc, x, other, offs, out):
         terms = held.tile([1, 2 * PITCH], F32, name="terms")
         nc.scalar.activation(terms[:, 0:E], miss_row[:, 0:E], ACT.Ln, bias=1.0, scale=-1.0)
 
-        d_others = psum.tile([1, N - E], F32, name="d_others")
-        nc.tensor.matmul(d_others[:], ones[:], products_others[:], start=True, stop=True)
-        nc.vector.tensor_scalar_mul(terms[:, PITCH : PITCH + E], d_others[:], -1.0)
+        minus_d_others = psum.tile([1, N - E], F32, name="minus_d_others")
+        nc.tensor.matmul(minus_d_others[:], ones[:], products_others[:], start=True, stop=True)
+        nc.vector.tensor_copy(terms[:, PITCH : PITCH + E], minus_d_others[:])
 
         nc.sync.dma_start(
             out.rearrange("o (h j) -> o h j", h=2),

@@ -34,8 +34,6 @@ def tile_graphloglikelihood_kernel(tc, x, other, offs, out):
 
         ones = held.tile([C, 1], F32, name="ones")
         nc.vector.memset(ones[:], 1.0)
-        warm = held.tile([C, 1], F32, name="warm")
-        nc.scalar.activation(warm[:], ones[:], ACT.Ln)
         inverse_e = held.tile([E, 1], F32, name="inverse_e")
         nc.vector.memset(inverse_e[:], 1.0 / math.e)
         miss = held.tile([P, 1], F32, name="miss")
@@ -67,7 +65,7 @@ def tile_graphloglikelihood_kernel(tc, x, other, offs, out):
                 d_edges[q : q + Q, :], products_edges[:, q : q + Q], ones[:], start=True, stop=True
             )
         d_edges_sbuf = held.tile([E, 1], F32, name="d_edges_sbuf")
-        nc.scalar.copy(d_edges_sbuf[:], d_edges[:])
+        nc.vector.tensor_copy(d_edges_sbuf[:], d_edges[:])
         nc.gpsimd.tensor_tensor(miss[0:E, :], inverse_e[:], d_edges_sbuf[:], ALU.pow)
         miss_row = psum.tile([1, P], F32, name="miss_row")
         nc.tensor.transpose(miss_row[:], miss[:], identity[:])

@@ -1,7 +1,6 @@
 import math
 
 import concourse.mybir as mybir
-from concourse.masks import make_identity
 
 F32 = mybir.dt.float32
 U16 = mybir.dt.uint16
@@ -14,7 +13,7 @@ N = 128
 E = 64
 P = 128
 Q = 32
-PITCH = 96
+PITCH = 48
 
 FLOPS = 2 * C * N
 
@@ -36,10 +35,8 @@ def tile_graphloglikelihood_kernel(tc, x, other, offs, out):
         nc.vector.memset(ones[:], 1.0)
         inverse_e = held.tile([E, 1], F32, name="inverse_e")
         nc.vector.memset(inverse_e[:], 1.0 / math.e)
-        miss = held.tile([P, 1], F32, name="miss")
+        miss = held.tile([P, Q], F32, name="miss", align_bytes=64)
         nc.vector.memset(miss[:], 0.0)
-        identity = held.tile([P, P], F32, name="identity")
-        make_identity(nc, identity[:])
 
         partners_negated = held.tile([C, N - E], F32, name="partners_negated")
         nc.vector.tensor_scalar_mul(partners_negated[:], partners[:, E:N], -1.0)
@@ -66,17 +63,22 @@ def tile_graphloglikelihood_kernel(tc, x, other, offs, out):
             )
         d_edges_sbuf = held.tile([E, 1], F32, name="d_edges_sbuf")
         nc.vector.tensor_copy(d_edges_sbuf[:], d_edges[:])
-        nc.gpsimd.tensor_tensor(miss[0:E, :], inverse_e[:], d_edges_sbuf[:], ALU.pow)
-        miss_row = psum.tile([1, P], F32, name="miss_row")
-        nc.tensor.transpose(miss_row[:], miss[:], identity[:])
-        terms = held.tile([1, 2 * PITCH], F32, name="terms")
-        nc.scalar.activation(terms[:, 0:E], miss_row[:, 0:E], ACT.Ln, bias=1.0, scale=-1.0)
+        nc.gpsimd.tensor_tensor(miss[0:E, 0:1], inverse_e[:], d_edges_sbuf[:], ALU.pow)
 
         minus_d_others = psum.tile([1, N - E], F32, name="minus_d_others")
         nc.tensor.matmul(minus_d_others[:], ones[:], products_others[:], start=True, stop=True)
-        nc.vector.tensor_copy(terms[:, PITCH : PITCH + E], minus_d_others[:])
-
+        terms_others = held.tile([1, (N - E) // Q, PITCH], F32, name="terms_others")
+        nc.vector.tensor_copy(
+            terms_others[:, :, 0:Q], minus_d_others[:].rearrange("o (h j) -> o h j", j=Q)
+        )
         nc.sync.dma_start(
-            out.rearrange("o (h j) -> o h j", h=2),
-            terms[:].rearrange("o (h w) -> o h w", h=2)[:, :, 0:E],
+            out[:, E:N].rearrange("o (h j) -> o h j", j=Q), terms_others[:, :, 0:Q]
+        )
+
+        miss_rows = held.tile([P, Q], F32, name="miss_rows", align_bytes=64)
+        nc.vector.transpose(miss_rows[:], miss[:])
+        terms_edges = held.tile([E, Q], F32, name="terms_edges")
+        nc.scalar.activation(terms_edges[:], miss_rows[0:E, :], ACT.Ln, bias=1.0, scale=-1.0)
+        nc.sync.dma_start(
+            out[:, 0:E].rearrange("o (h j) -> (o h) j", j=Q), terms_edges[0:E:Q, :]
         )

import math

import concourse.mybir as mybir

F32 = mybir.dt.float32
U16 = mybir.dt.uint16
ACT = mybir.ActivationFunctionType
ALU = mybir.AluOpType

C = 128
S = 1024
N = 128
E = 64
P = 128
Q = 32
PITCH = 48

FLOPS = 2 * C * N


def tile_graphloglikelihood_kernel(tc, x, other, offs, out):
    nc = tc.nc
    with (
        tc.tile_pool(name="held", bufs=1) as held,
        tc.psum_pool(name="psum", bufs=1) as psum,
    ):
        nodes = held.tile([C, S], F32, name="nodes")
        nc.scalar.dma_start(nodes[:], x)
        partners = held.tile([C, N], F32, name="partners")
        nc.sync.dma_start(partners[:], other)
        offsets = held.tile([C, N // 16], U16, name="offsets")
        nc.sync.dma_start(offsets[:], offs)

        ones = held.tile([C, 1], F32, name="ones")
        nc.vector.memset(ones[:], 1.0)
        inverse_e = held.tile([E, 1], F32, name="inverse_e")
        nc.vector.memset(inverse_e[:], 1.0 / math.e)
        miss = held.tile([P, Q], F32, name="miss", align_bytes=64)
        nc.vector.memset(miss[:], 0.0)

        partners_negated = held.tile([C, N - E], F32, name="partners_negated")
        nc.vector.tensor_scalar_mul(partners_negated[:], partners[:, E:N], -1.0)

        products_edges = held.tile([C, E], F32, name="products_edges")
        nc.vector.tensor_tensor(
            products_edges[:],
            nodes[:].indirect(offsets[:, 0 : E // 16]),
            partners[:, 0:E],
            ALU.mult,
        )
        products_others = held.tile([C, N - E], F32, name="products_others")
        nc.vector.tensor_tensor(
            products_others[:],
            nodes[:].indirect(offsets[:, E // 16 : N // 16]),
            partners_negated[:],
            ALU.mult,
        )

        d_edges = psum.tile([E, 1], F32, name="d_edges")
        for q in range(0, E, Q):
            nc.tensor.matmul(
                d_edges[q : q + Q, :], products_edges[:, q : q + Q], ones[:], start=True, stop=True
            )
        d_edges_sbuf = held.tile([E, 1], F32, name="d_edges_sbuf")
        nc.vector.tensor_copy(d_edges_sbuf[:], d_edges[:])
        nc.gpsimd.tensor_tensor(miss[0:E, 0:1], inverse_e[:], d_edges_sbuf[:], ALU.pow)

        minus_d_others = psum.tile([1, N - E], F32, name="minus_d_others")
        nc.tensor.matmul(minus_d_others[:], ones[:], products_others[:], start=True, stop=True)
        terms_others = held.tile([1, (N - E) // Q, PITCH], F32, name="terms_others")
        nc.vector.tensor_copy(
            terms_others[:, :, 0:Q], minus_d_others[:].rearrange("o (h j) -> o h j", j=Q)
        )
        nc.sync.dma_start(
            out[:, E:N].rearrange("o (h j) -> o h j", j=Q), terms_others[:, :, 0:Q]
        )

        miss_rows = held.tile([P, Q], F32, name="miss_rows", align_bytes=64)
        nc.vector.transpose(miss_rows[:], miss[:])
        terms_edges = held.tile([E, Q], F32, name="terms_edges")
        nc.scalar.activation(terms_edges[:], miss_rows[0:E, :], ACT.Ln, bias=1.0, scale=-1.0)
        nc.sync.dma_start(
            out[:, 0:E].rearrange("o (h j) -> (o h) j", j=Q), terms_edges[0:E:Q, :]
        )
